import numpy as np
import ml_dtypes


def mxq(x, axis, fmt="e4m3"):
    dtype, down = {"e4m3": (ml_dtypes.float8_e4m3fn, 7), "e5m2": (ml_dtypes.float8_e5m2, 14)}[fmt]
    v = np.moveaxis(np.asarray(x, np.float32).astype(ml_dtypes.bfloat16).astype(np.float64), axis, -1)
    blocks = v.reshape(v.shape[:-1] + (-1, 32))
    amax = np.abs(blocks).max(-1, keepdims=True)
    byte = np.maximum(np.where(amax > 0, np.frexp(amax)[1] - 1 + 127, 0) - down, 1)
    scale = np.exp2(byte - 127.0)
    codes = (blocks / scale).astype(np.float32).astype(dtype).astype(np.float64)
    return np.moveaxis((codes * scale).reshape(v.shape), -1, axis)


WIDE = False


def mx_kscale(k):
    if not WIDE:
        return np.ones(k)
    levels = np.array([10, -10, 5, -5, 0])
    a = np.random.permutation(np.resize(levels, k // 512 * 4)).reshape(k // 512, 4)
    idx = np.arange(k)
    return np.exp2(a[idx // 512, idx % 128 // 32])


BF16 = ml_dtypes.bfloat16


def bf(x):
    return np.asarray(x, np.float32).astype(BF16)


def f64(x):
    return np.asarray(x).astype(np.float64)


B, T, D, H, F = 4, 1024, 512, 8, 512


def erf(z):
    a = np.minimum(np.abs(z), 6.0)
    y = 2.0 * a * a
    term = a.copy()
    total = a.copy()
    n = 0.0
    while np.any(term > 1e-18 * total):
        n += 1.0
        term = term * (y / (2.0 * n + 1.0))
        total = total + term
    return np.sign(z) * (2.0 / np.sqrt(np.pi)) * np.exp(-a * a) * total


def gelu_erf(v):
    return 0.5 * v * (1.0 + erf(v / np.sqrt(2.0)))


def setup_inputs():
    s = mx_kscale(D)
    return {
        "x": bf(np.random.standard_normal((B, T, D))),
        "attn_merged": bf(np.random.standard_normal((B, T, D)) * 0.6 * s),
        "w_proj": bf(np.random.standard_normal((D, D)) * 1.5 / np.sqrt(D) / s[:, None]),
        "w_ff1": bf(np.random.standard_normal((D, F)) / np.sqrt(D)),
        "b_ff1": bf(np.random.standard_normal(F) * 0.3),
        "w_ff2": bf(np.random.standard_normal((F, D)) * 1.5 / np.sqrt(F)),
        "b_ff2": bf(np.random.standard_normal(D) * 0.3),
    }


def reference(x, attn_merged, w_proj, w_ff1, b_ff1, w_ff2, b_ff2):
    x = f64(x)
    attn_out = mxq(f64(attn_merged), 2, "e4m3") @ mxq(f64(w_proj), 0, "e4m3")
    h = gelu_erf((mxq(x, 2, "e4m3") @ mxq(f64(w_ff1), 0, "e4m3")) + f64(b_ff1))
    ff_out = (mxq(h, 2, "e4m3") @ mxq(f64(w_ff2), 0, "e4m3")) + f64(b_ff2)
    return x + attn_out + ff_out

@@ -1,0 +1,270 @@
+from contextlib import ExitStack
+
+import concourse.mybir as mybir
+from concourse.masks import make_identity
+
+F32 = mybir.dt.float32
+BF16 = mybir.dt.bfloat16
+I32 = mybir.dt.int32
+U32 = mybir.dt.uint32
+U8 = mybir.dt.uint8
+FP8X4 = mybir.dt.float8_e4m3fn_x4
+GELU = mybir.ActivationFunctionType.Gelu
+ADD = mybir.AluOpType.add
+
+P = 128
+PACK = 4
+WIDTH = P * PACK
+TOKENS = 4 * 1024
+TILES = 4
+ROUND = TILES * P
+ROUNDS = TOKENS // ROUND
+HALF = WIDTH // 2
+FLOPS = 3 * 2 * TOKENS * WIDTH * WIDTH
+
+
+def tile_block_pa_t_kernel(
+    tc, x, attn_merged, w_proj, w_ff1, b_ff1, w_ff2, b_ff2, out
+):
+    nc = tc.nc
+
+    by_round = "(r p i) d -> r p (i d)"
+    x_dram = x.flatten_outer_dims().rearrange(by_round, p=P, i=TILES)
+    a_dram = attn_merged.flatten_outer_dims().rearrange(by_round, p=P, i=TILES)
+    out_dram = out.flatten_outer_dims().rearrange(by_round, p=P, i=TILES)
+
+    with ExitStack() as ctx:
+        keep = ctx.enter_context(tc.tile_pool(name="keep", bufs=1))
+        two = ctx.enter_context(tc.tile_pool(name="two", bufs=2))
+        three = ctx.enter_context(tc.tile_pool(name="three", bufs=3))
+        psum = ctx.enter_context(tc.psum_pool(name="psum", bufs=8))
+        ctx.enter_context(tc.manual_schedule())
+
+        def bank(name):
+            return psum.tile([P, WIDTH], F32, name=name, tag="bank")
+
+        x_sb = [keep.tile([P, TILES * WIDTH], BF16, name="x%d" % r) for r in range(ROUNDS)]
+        a_sb = [keep.tile([P, TILES * WIDTH], BF16, name="a%d" % r) for r in range(ROUNDS)]
+        w1_raw = keep.tile([P, PACK, WIDTH], BF16)
+        wp_raw = keep.tile([P, PACK, WIDTH], BF16)
+        w2_raw = keep.tile([P, PACK, WIDTH], BF16)
+
+        pairs_dram = "(u p e) c -> p u (e c)"
+        pairs_sbuf = "p (u e) c -> p u (e c)"
+        nc.sync.dma_start(out=x_sb[0][:], in_=x_dram[0])
+        nc.sync.dma_start(
+            out=w1_raw[:].rearrange(pairs_sbuf, u=2), in_=w_ff1.rearrange(pairs_dram, u=2, e=2)
+        )
+        nc.sync.dma_start(out=a_sb[0][:], in_=a_dram[0])
+        nc.sync.dma_start(
+            out=wp_raw[:].rearrange(pairs_sbuf, u=2), in_=w_proj.rearrange(pairs_dram, u=2, e=2)
+        )
+        nc.sync.dma_start(
+            out=w2_raw[:].rearrange("p s c -> p (s c)"),
+            in_=w_ff2.rearrange("(p s) c -> p (s c)", s=PACK),
+        )
+        for r in range(1, ROUNDS):
+            nc.sync.dma_start(out=x_sb[r][:], in_=x_dram[r])
+            nc.sync.dma_start(out=a_sb[r][:], in_=a_dram[r])
+
+        b1_bf16 = keep.tile([P, PACK], BF16)
+        b1 = keep.tile([P, PACK], F32)
+        nc.scalar.dma_start(out=b1_bf16[:], in_=b_ff1.rearrange("(p s) -> p s", s=PACK))
+
+        ones = keep.tile([P, P], BF16)
+        b2_rows = keep.tile([P, WIDTH], BF16)
+        b2_all = keep.tile([P, WIDTH], BF16)
+        nc.vector.memset(b2_rows[:].bitcast(I32), 0)
+        nc.vector.memset(ones[:], 1.0)
+        nc.scalar.dma_start(out=b2_rows[0:1, :], in_=b_ff2.unsqueeze(0))
+
+        warm = keep.tile([P, 1], F32)
+        warm_out = keep.tile([P, 1], F32)
+        nc.vector.memset(warm[:], 0.0)
+        nc.scalar.activation(out=warm_out[:], in_=warm[:], func=GELU)
+
+        b2_bank = bank("b2_bank")
+        nc.tensor.matmul(out=b2_bank[:], lhsT=ones[:], rhs=b2_rows[:], start=True, stop=True)
+        nc.scalar.copy(out=b2_all[:], in_=b2_bank[:])
+
+        ident = keep.tile([P, P], F32)
+        make_identity(nc, ident[:])
+
+        def quantise_weight(raw_view, name):
+            grouped = two.tile([P, WIDTH, PACK], BF16, align_bytes=64, name="w_grouped")
+            codes = keep.tile([P, WIDTH], U32, align_bytes=64, name=name + "_codes")
+            scales = keep.tile([P, WIDTH], U8, align_bytes=64, name=name + "_scales")
+            nc.vector.tensor_copy(
+                out=grouped[:].rearrange("p (a b) j -> p a b j", a=PACK), in_=raw_view
+            )
+            nc.vector.quantize_mx(
+                out=codes[:].bitcast(FP8X4),
+                scales=scales[:],
+                in_=grouped[:].rearrange("p c j -> p (c j)"),
+            )
+            return codes, scales
+
+        w1_codes, w1_scales = quantise_weight(
+            w1_raw[:].rearrange("p j (m s) -> p s m j", s=PACK), "w1"
+        )
+
+        transposed = {}
+        xa_grouped = {}
+        xa_codes = {}
+        xa_scales = {}
+        h_banks = {}
+        h_planes = {}
+        h_grouped = {}
+        h_codes = {}
+        h_scales = {}
+        out_banks = {}
+        resid = {}
+
+        def transpose_round(r):
+            transposed[r] = []
+            for src in (x_sb[r], a_sb[r]):
+                for half in range(2):
+                    words_t = bank("words_t")
+                    for i in range(2):
+                        tile_i = 2 * half + i
+                        words = src[:, tile_i * WIDTH : (tile_i + 1) * WIDTH].bitcast(F32)
+                        for u in range(2):
+                            nc.tensor.transpose(
+                                out=words_t[:, u * HALF + i * P : u * HALF + (i + 1) * P],
+                                in_=words[:, u * P : (u + 1) * P],
+                                identity=ident[:],
+                            )
+                    transposed[r].append(words_t)
+
+        def regroup_round(r):
+            grouped = two.tile([P, 2 * ROUND * PACK], BF16, align_bytes=64, name="xa_grouped")
+            for j, words_t in enumerate(transposed[r]):
+                nc.scalar.copy(
+                    out=grouped[:, j * 2 * WIDTH : (j + 1) * 2 * WIDTH]
+                    .bitcast(F32)
+                    .rearrange("p (c u) -> p c u", u=2),
+                    in_=words_t[:].rearrange("p (u c) -> p c u", u=2),
+                )
+            xa_grouped[r] = grouped
+
+        def quantise_round(r):
+            codes = three.tile([P, 2 * ROUND], U32, align_bytes=64, name="xa_codes")
+            scales = three.tile([P, 2 * ROUND], U8, align_bytes=64, name="xa_scales")
+            nc.vector.quantize_mx(
+                out=codes[:].bitcast(FP8X4), scales=scales[:], in_=xa_grouped[r][:]
+            )
+            xa_codes[r] = codes
+            xa_scales[r] = scales
+
+        def hidden_matmuls(r):
+            h_banks[r] = []
+            for s in range(PACK):
+                h_bank = bank("h_bank")
+                nc.tensor.matmul_mx(
+                    out=h_bank[:],
+                    lhsT=w1_codes[:, s * P : (s + 1) * P].bitcast(FP8X4),
+                    lhsT_scale=w1_scales[:, s * P : (s + 1) * P],
+                    rhs=xa_codes[r][:, 0:ROUND].bitcast(FP8X4),
+                    rhs_scale=xa_scales[r][:, 0:ROUND],
+                    start=True,
+                    stop=True,
+                )
+                h_banks[r].append(h_bank)
+
+        def gelu_round(r):
+            planes = two.tile([P, PACK, ROUND], BF16, name="h_planes")
+            for s in range(PACK):
+                nc.scalar.activation(
+                    out=planes[:, s, :], in_=h_banks[r][s][:], func=GELU, bias=b1[:, s : s + 1]
+                )
+            h_planes[r] = planes
+
+        def regroup_hidden(r):
+            grouped = two.tile([P, ROUND, PACK], BF16, align_bytes=64, name="h_grouped")
+            nc.scalar.copy(
+                out=grouped[:].rearrange("p (c i) s -> p c s i", i=4),
+                in_=h_planes[r][:].rearrange("p s (c i) -> p c s i", i=4),
+            )
+            h_grouped[r] = grouped
+
+        def quantise_hidden(r):
+            codes = two.tile([P, ROUND], U32, align_bytes=64, name="h_codes")
+            scales = two.tile([P, ROUND], U8, align_bytes=64, name="h_scales")
+            nc.vector.quantize_mx(
+                out=codes[:].bitcast(FP8X4),
+                scales=scales[:],
+                in_=h_grouped[r][:].rearrange("p c s -> p (c s)"),
+            )
+            h_codes[r] = codes
+            h_scales[r] = scales
+
+        def residual_round(r):
+            xb = keep.tile([P, TILES, WIDTH], F32, name="resid%d" % r)
+            nc.vector.tensor_tensor(
+                out=xb[:],
+                in0=x_sb[r][:].rearrange("p (i d) -> p i d", i=TILES),
+                in1=b2_all[:].unsqueeze(1).to_broadcast([P, TILES, WIDTH]),
+                op=ADD,
+            )
+            resid[r] = xb
+
+        def output_matmuls(r):
+            out_banks[r] = []
+            for i in range(TILES):
+                out_bank = bank("out_bank")
+                nc.tensor.matmul_mx(
+                    out=out_bank[:],
+                    lhsT=xa_codes[r][:, ROUND + i * P : ROUND + (i + 1) * P].bitcast(FP8X4),
+                    lhsT_scale=xa_scales[r][:, ROUND + i * P : ROUND + (i + 1) * P],
+                    rhs=wp_codes[:].bitcast(FP8X4),
+                    rhs_scale=wp_scales[:],
+                    start=True,
+                    stop=False,
+                )
+                nc.tensor.matmul_mx(
+                    out=out_bank[:],
+                    lhsT=h_codes[r][:, i * P : (i + 1) * P].bitcast(FP8X4),
+                    lhsT_scale=h_scales[r][:, i * P : (i + 1) * P],
+                    rhs=w2_codes[:].bitcast(FP8X4),
+                    rhs_scale=w2_scales[:],
+                    start=False,
+                    stop=True,
+                )
+                out_banks[r].append(out_bank)
+
+        def finish_round(r):
+            for i in range(TILES):
+                nc.vector.tensor_tensor(
+                    out=resid[r][:, i, :], in0=out_banks[r][i][:], in1=resid[r][:, i, :], op=ADD
+                )
+            nc.sync.dma_start(out=out_dram[r], in_=resid[r][:].rearrange("p i d -> p (i d)"))
+
+        transpose_round(0)
+        regroup_round(0)
+        quantise_round(0)
+        nc.vector.tensor_copy(out=b1[:], in_=b1_bf16[:])
+        wp_codes, wp_scales = quantise_weight(
+            wp_raw[:].rearrange("p j (a b) -> p a b j", a=PACK), "wp"
+        )
+        w2_codes, w2_scales = quantise_weight(
+            w2_raw[:].rearrange("p j (a b) -> p a b j", a=PACK), "w2"
+        )
+        residual_round(0)
+
+        for n in range(ROUNDS + 1):
+            if n >= 1:
+                quantise_hidden(n - 1)
+            if n < ROUNDS:
+                hidden_matmuls(n)
+                gelu_round(n)
+            if n + 1 < ROUNDS:
+                transpose_round(n + 1)
+                residual_round(n + 1)
+                regroup_round(n + 1)
+            if n >= 1:
+                output_matmuls(n - 1)
+                finish_round(n - 1)
+            if n < ROUNDS:
+                regroup_hidden(n)
+            if n + 1 < ROUNDS:
+                quantise_round(n + 1)

@@ -83,46 +83,35 @@ def tile_block_pa_t_kernel(
         nc.vector.memset(warm[:], 0.0)
         nc.scalar.activation(out=warm_out[:], in_=warm[:], func=GELU)
 
-        b2_bank = bank("b2_bank")
-        nc.tensor.matmul(out=b2_bank[:], lhsT=ones[:], rhs=b2_rows[:], start=True, stop=True)
-        nc.scalar.copy(out=b2_all[:], in_=b2_bank[:])
-
         ident = keep.tile([P, P], F32)
         make_identity(nc, ident[:])
 
         def quantise_weight(raw_view, name):
-            grouped = two.tile([P, WIDTH, PACK], BF16, align_bytes=64, name="w_grouped")
+            w_grouped = two.tile([P, WIDTH, PACK], BF16, align_bytes=64)
             codes = keep.tile([P, WIDTH], U32, align_bytes=64, name=name + "_codes")
             scales = keep.tile([P, WIDTH], U8, align_bytes=64, name=name + "_scales")
             nc.vector.tensor_copy(
-                out=grouped[:].rearrange("p (a b) j -> p a b j", a=PACK), in_=raw_view
+                out=w_grouped[:].rearrange("p (a b) j -> p a b j", a=PACK), in_=raw_view
             )
             nc.vector.quantize_mx(
                 out=codes[:].bitcast(FP8X4),
                 scales=scales[:],
-                in_=grouped[:].rearrange("p c j -> p (c j)"),
+                in_=w_grouped[:].rearrange("p c j -> p (c j)"),
             )
             return codes, scales
 
-        w1_codes, w1_scales = quantise_weight(
-            w1_raw[:].rearrange("p j (m s) -> p s m j", s=PACK), "w1"
-        )
-
         transposed = {}
-        xa_grouped = {}
-        xa_codes = {}
-        xa_scales = {}
+        grouped = {}
+        codes = {}
+        scales = {}
         h_banks = {}
         h_planes = {}
-        h_grouped = {}
-        h_codes = {}
-        h_scales = {}
         out_banks = {}
         resid = {}
 
         def transpose_round(r):
-            transposed[r] = []
-            for src in (x_sb[r], a_sb[r]):
+            for name, src in (("x", x_sb[r]), ("a", a_sb[r])):
+                transposed[name, r] = []
                 for half in range(2):
                     words_t = bank("words_t")
                     for i in range(2):
@@ -134,27 +123,32 @@ def tile_block_pa_t_kernel(
                                 in_=words[:, u * P : (u + 1) * P],
                                 identity=ident[:],
                             )
-                    transposed[r].append(words_t)
+                    transposed[name, r].append(words_t)
 
         def regroup_round(r):
-            grouped = two.tile([P, 2 * ROUND * PACK], BF16, align_bytes=64, name="xa_grouped")
-            for j, words_t in enumerate(transposed[r]):
-                nc.scalar.copy(
-                    out=grouped[:, j * 2 * WIDTH : (j + 1) * 2 * WIDTH]
-                    .bitcast(F32)
-                    .rearrange("p (c u) -> p c u", u=2),
-                    in_=words_t[:].rearrange("p (u c) -> p c u", u=2),
-                )
-            xa_grouped[r] = grouped
+            for name in ("x", "a"):
+                side = two.tile([P, ROUND * PACK], BF16, align_bytes=64, name=name + "_grouped")
+                for half, words_t in enumerate(transposed[name, r]):
+                    nc.scalar.copy(
+                        out=side[:, half * 2 * WIDTH : (half + 1) * 2 * WIDTH]
+                        .bitcast(F32)
+                        .rearrange("p (c u) -> p c u", u=2),
+                        in_=words_t[:].rearrange("p (u c) -> p c u", u=2),
+                    )
+                grouped[name, r] = side
 
-        def quantise_round(r):
-            codes = three.tile([P, 2 * ROUND], U32, align_bytes=64, name="xa_codes")
-            scales = three.tile([P, 2 * ROUND], U8, align_bytes=64, name="xa_scales")
-            nc.vector.quantize_mx(
-                out=codes[:].bitcast(FP8X4), scales=scales[:], in_=xa_grouped[r][:]
-            )
-            xa_codes[r] = codes
-            xa_scales[r] = scales
+        def quantise(name, r, pieces):
+            code = three.tile([P, ROUND], U32, align_bytes=64, name=name + "_codes")
+            scale = three.tile([P, ROUND], U8, align_bytes=64, name=name + "_scales")
+            step = ROUND // pieces
+            for c in range(0, ROUND, step):
+                nc.vector.quantize_mx(
+                    out=code[:, c : c + step].bitcast(FP8X4),
+                    scales=scale[:, c : c + step],
+                    in_=grouped[name, r][:, c * PACK : (c + step) * PACK],
+                )
+            codes[name, r] = code
+            scales[name, r] = scale
 
         def hidden_matmuls(r):
             h_banks[r] = []
@@ -164,8 +158,8 @@ def tile_block_pa_t_kernel(
                     out=h_bank[:],
                     lhsT=w1_codes[:, s * P : (s + 1) * P].bitcast(FP8X4),
                     lhsT_scale=w1_scales[:, s * P : (s + 1) * P],
-                    rhs=xa_codes[r][:, 0:ROUND].bitcast(FP8X4),
-                    rhs_scale=xa_scales[r][:, 0:ROUND],
+                    rhs=codes["x", r][:].bitcast(FP8X4),
+                    rhs_scale=scales["x", r][:],
                     start=True,
                     stop=True,
                 )
@@ -180,26 +174,20 @@ def tile_block_pa_t_kernel(
             h_planes[r] = planes
 
         def regroup_hidden(r):
-            grouped = two.tile([P, ROUND, PACK], BF16, align_bytes=64, name="h_grouped")
-            nc.scalar.copy(
-                out=grouped[:].rearrange("p (c i) s -> p c s i", i=4),
-                in_=h_planes[r][:].rearrange("p s (c i) -> p c s i", i=4),
-            )
-            h_grouped[r] = grouped
-
-        def quantise_hidden(r):
-            codes = two.tile([P, ROUND], U32, align_bytes=64, name="h_codes")
-            scales = two.tile([P, ROUND], U8, align_bytes=64, name="h_scales")
-            nc.vector.quantize_mx(
-                out=codes[:].bitcast(FP8X4),
-                scales=scales[:],
-                in_=h_grouped[r][:].rearrange("p c s -> p (c s)"),
-            )
-            h_codes[r] = codes
-            h_scales[r] = scales
+            side = two.tile([P, ROUND * PACK], BF16, align_bytes=64, name="h_grouped")
+            for c in range(0, ROUND, ROUND // 2):
+                nc.scalar.copy(
+                    out=side[:, c * PACK : (c + ROUND // 2) * PACK].rearrange(
+                        "p (c i s) -> p c s i", i=4, s=PACK
+                    ),
+                    in_=h_planes[r][:, :, c : c + ROUND // 2].rearrange(
+                        "p s (c i) -> p c s i", i=4
+                    ),
+                )
+            grouped["h", r] = side
 
         def residual_round(r):
-            xb = keep.tile([P, TILES, WIDTH], F32, name="resid%d" % r)
+            xb = three.tile([P, TILES, WIDTH], F32, name="resid")
             nc.vector.tensor_tensor(
                 out=xb[:],
                 in0=x_sb[r][:].rearrange("p (i d) -> p i d", i=TILES),
@@ -211,11 +199,12 @@ def tile_block_pa_t_kernel(
         def output_matmuls(r):
             out_banks[r] = []
             for i in range(TILES):
+                tile_cols = slice(i * P, (i + 1) * P)
                 out_bank = bank("out_bank")
                 nc.tensor.matmul_mx(
                     out=out_bank[:],
-                    lhsT=xa_codes[r][:, ROUND + i * P : ROUND + (i + 1) * P].bitcast(FP8X4),
-                    lhsT_scale=xa_scales[r][:, ROUND + i * P : ROUND + (i + 1) * P],
+                    lhsT=codes["a", r][:, tile_cols].bitcast(FP8X4),
+                    lhsT_scale=scales["a", r][:, tile_cols],
                     rhs=wp_codes[:].bitcast(FP8X4),
                     rhs_scale=wp_scales[:],
                     start=True,
@@ -223,8 +212,8 @@ def tile_block_pa_t_kernel(
                 )
                 nc.tensor.matmul_mx(
                     out=out_bank[:],
-                    lhsT=h_codes[r][:, i * P : (i + 1) * P].bitcast(FP8X4),
-                    lhsT_scale=h_scales[r][:, i * P : (i + 1) * P],
+                    lhsT=codes["h", r][:, tile_cols].bitcast(FP8X4),
+                    lhsT_scale=scales["h", r][:, tile_cols],
                     rhs=w2_codes[:].bitcast(FP8X4),
                     rhs_scale=w2_scales[:],
                     start=False,
@@ -237,34 +226,47 @@ def tile_block_pa_t_kernel(
                 nc.vector.tensor_tensor(
                     out=resid[r][:, i, :], in0=out_banks[r][i][:], in1=resid[r][:, i, :], op=ADD
                 )
-            nc.sync.dma_start(out=out_dram[r], in_=resid[r][:].rearrange("p i d -> p (i d)"))
+                if i % 2 == 1:
+                    nc.sync.dma_start(
+                        out=out_dram[r][:, (i - 1) * WIDTH : (i + 1) * WIDTH],
+                        in_=resid[r][:, i - 1 : i + 1, :].rearrange("p i d -> p (i d)"),
+                    )
 
         transpose_round(0)
+        b2_bank = bank("b2_bank")
+        nc.tensor.matmul(out=b2_bank[:], lhsT=ones[:], rhs=b2_rows[:], start=True, stop=True)
+        w1_codes, w1_scales = quantise_weight(
+            w1_raw[:].rearrange("p j (m s) -> p s m j", s=PACK), "w1"
+        )
         regroup_round(0)
-        quantise_round(0)
+        nc.scalar.copy(out=b2_all[:], in_=b2_bank[:])
+        quantise("x", 0, 1)
         nc.vector.tensor_copy(out=b1[:], in_=b1_bf16[:])
+        quantise("a", 0, 1)
         wp_codes, wp_scales = quantise_weight(
             wp_raw[:].rearrange("p j (a b) -> p a b j", a=PACK), "wp"
         )
         w2_codes, w2_scales = quantise_weight(
             w2_raw[:].rearrange("p j (a b) -> p a b j", a=PACK), "w2"
         )
-        residual_round(0)
 
         for n in range(ROUNDS + 1):
             if n >= 1:
-                quantise_hidden(n - 1)
+                quantise("h", n - 1, 2)
             if n < ROUNDS:
                 hidden_matmuls(n)
                 gelu_round(n)
             if n + 1 < ROUNDS:
                 transpose_round(n + 1)
-                residual_round(n + 1)
                 regroup_round(n + 1)
+            if n >= 1:
+                residual_round(n - 1)
+            if n + 1 < ROUNDS:
+                quantise("x", n + 1, 1)
             if n >= 1:
                 output_matmuls(n - 1)
                 finish_round(n - 1)
             if n < ROUNDS:
                 regroup_hidden(n)
             if n + 1 < ROUNDS:
-                quantise_round(n + 1)
+                quantise("a", n + 1, 1)

@@ -125,17 +125,17 @@ def tile_block_pa_t_kernel(
                             )
                     transposed[name, r].append(words_t)
 
-        def regroup_round(r):
-            for name in ("x", "a"):
-                side = two.tile([P, ROUND * PACK], BF16, align_bytes=64, name=name + "_grouped")
-                for half, words_t in enumerate(transposed[name, r]):
-                    nc.scalar.copy(
-                        out=side[:, half * 2 * WIDTH : (half + 1) * 2 * WIDTH]
-                        .bitcast(F32)
-                        .rearrange("p (c u) -> p c u", u=2),
-                        in_=words_t[:].rearrange("p (u c) -> p c u", u=2),
-                    )
-                grouped[name, r] = side
+        def regroup(name, r):
+            side = two.tile([P, ROUND * PACK], BF16, align_bytes=64, name=name + "_grouped")
+            for half, words_t in enumerate(transposed[name, r]):
+                copy = nc.vector.tensor_copy if (name, half) == ("x", 1) else nc.scalar.copy
+                copy(
+                    out=side[:, half * 2 * WIDTH : (half + 1) * 2 * WIDTH]
+                    .bitcast(F32)
+                    .rearrange("p (c u) -> p c u", u=2),
+                    in_=words_t[:].rearrange("p (u c) -> p c u", u=2),
+                )
+            grouped[name, r] = side
 
         def quantise(name, r, pieces):
             code = three.tile([P, ROUND], U32, align_bytes=64, name=name + "_codes")
@@ -187,13 +187,14 @@ def tile_block_pa_t_kernel(
             grouped["h", r] = side
 
         def residual_round(r):
-            xb = three.tile([P, TILES, WIDTH], F32, name="resid")
-            nc.vector.tensor_tensor(
-                out=xb[:],
-                in0=x_sb[r][:].rearrange("p (i d) -> p i d", i=TILES),
-                in1=b2_all[:].unsqueeze(1).to_broadcast([P, TILES, WIDTH]),
-                op=ADD,
-            )
+            xb = keep.tile([P, TILES, WIDTH], F32, name="resid%d" % r)
+            for i in range(TILES):
+                nc.gpsimd.tensor_tensor(
+                    out=xb[:, i, :],
+                    in0=x_sb[r][:, i * WIDTH : (i + 1) * WIDTH],
+                    in1=b2_all[:],
+                    op=ADD,
+                )
             resid[r] = xb
 
         def output_matmuls(r):
@@ -238,11 +239,14 @@ def tile_block_pa_t_kernel(
         w1_codes, w1_scales = quantise_weight(
             w1_raw[:].rearrange("p j (m s) -> p s m j", s=PACK), "w1"
         )
-        regroup_round(0)
-        nc.scalar.copy(out=b2_all[:], in_=b2_bank[:])
+        regroup("x", 0)
         quantise("x", 0, 1)
         nc.vector.tensor_copy(out=b1[:], in_=b1_bf16[:])
+        regroup("a", 0)
         quantise("a", 0, 1)
+        nc.scalar.copy(out=b2_all[:], in_=b2_bank[:])
+        for r in range(ROUNDS):
+            residual_round(r)
         wp_codes, wp_scales = quantise_weight(
             wp_raw[:].rearrange("p j (a b) -> p a b j", a=PACK), "wp"
         )
@@ -258,11 +262,9 @@ def tile_block_pa_t_kernel(
                 gelu_round(n)
             if n + 1 < ROUNDS:
                 transpose_round(n + 1)
-                regroup_round(n + 1)
-            if n >= 1:
-                residual_round(n - 1)
-            if n + 1 < ROUNDS:
+                regroup("x", n + 1)
                 quantise("x", n + 1, 1)
+                regroup("a", n + 1)
             if n >= 1:
                 output_matmuls(n - 1)
                 finish_round(n - 1)

@@ -186,9 +186,9 @@ def tile_block_pa_t_kernel(
                 )
             grouped["h", r] = side
 
-        def residual_round(r):
+        def residual_gpsimd(r):
             xb = keep.tile([P, TILES, WIDTH], F32, name="resid%d" % r)
-            for i in range(TILES):
+            for i in range(TILES // 2, TILES):
                 nc.gpsimd.tensor_tensor(
                     out=xb[:, i, :],
                     in0=x_sb[r][:, i * WIDTH : (i + 1) * WIDTH],
@@ -196,6 +196,14 @@ def tile_block_pa_t_kernel(
                     op=ADD,
                 )
             resid[r] = xb
+
+        def residual_vector(r):
+            nc.vector.tensor_tensor(
+                out=resid[r][:, 0 : TILES // 2, :],
+                in0=x_sb[r][:, 0 : TILES // 2 * WIDTH].rearrange("p (i d) -> p i d", d=WIDTH),
+                in1=b2_all[:].unsqueeze(1).to_broadcast([P, TILES // 2, WIDTH]),
+                op=ADD,
+            )
 
         def output_matmuls(r):
             out_banks[r] = []
@@ -246,7 +254,7 @@ def tile_block_pa_t_kernel(
         quantise("a", 0, 1)
         nc.scalar.copy(out=b2_all[:], in_=b2_bank[:])
         for r in range(ROUNDS):
-            residual_round(r)
+            residual_gpsimd(r)
         wp_codes, wp_scales = quantise_weight(
             wp_raw[:].rearrange("p j (a b) -> p a b j", a=PACK), "wp"
         )
@@ -257,6 +265,7 @@ def tile_block_pa_t_kernel(
         for n in range(ROUNDS + 1):
             if n >= 1:
                 quantise("h", n - 1, 2)
+                residual_vector(n - 1)
             if n < ROUNDS:
                 hidden_matmuls(n)
                 gelu_round(n)

@@ -128,8 +128,7 @@ def tile_block_pa_t_kernel(
         def regroup(name, r):
             side = two.tile([P, ROUND * PACK], BF16, align_bytes=64, name=name + "_grouped")
             for half, words_t in enumerate(transposed[name, r]):
-                copy = nc.vector.tensor_copy if (name, half) == ("x", 1) else nc.scalar.copy
-                copy(
+                nc.scalar.copy(
                     out=side[:, half * 2 * WIDTH : (half + 1) * 2 * WIDTH]
                     .bitcast(F32)
                     .rearrange("p (c u) -> p c u", u=2),
@@ -175,8 +174,8 @@ def tile_block_pa_t_kernel(
 
         def regroup_hidden(r):
             side = two.tile([P, ROUND * PACK], BF16, align_bytes=64, name="h_grouped")
-            for c in range(0, ROUND, ROUND // 2):
-                nc.scalar.copy(
+            for c, copy in ((0, nc.scalar.copy), (ROUND // 2, nc.vector.tensor_copy)):
+                copy(
                     out=side[:, c * PACK : (c + ROUND // 2) * PACK].rearrange(
                         "p (c i s) -> p c s i", i=4, s=PACK
                     ),

@@ -51,10 +51,10 @@ def tile_block_pa_t_kernel(
 
         pairs_dram = "(u p e) c -> p u (e c)"
         pairs_sbuf = "p (u e) c -> p u (e c)"
-        nc.sync.dma_start(out=x_sb[0][:], in_=x_dram[0])
         nc.sync.dma_start(
             out=w1_raw[:].rearrange(pairs_sbuf, u=2), in_=w_ff1.rearrange(pairs_dram, u=2, e=2)
         )
+        nc.sync.dma_start(out=x_sb[0][:], in_=x_dram[0])
         nc.sync.dma_start(out=a_sb[0][:], in_=a_dram[0])
         nc.sync.dma_start(
             out=wp_raw[:].rearrange(pairs_sbuf, u=2), in_=w_proj.rearrange(pairs_dram, u=2, e=2)
@@ -174,7 +174,8 @@ def tile_block_pa_t_kernel(
 
         def regroup_hidden(r):
             side = two.tile([P, ROUND * PACK], BF16, align_bytes=64, name="h_grouped")
-            for c, copy in ((0, nc.scalar.copy), (ROUND // 2, nc.vector.tensor_copy)):
+            second = nc.vector.tensor_copy if r + 1 < ROUNDS else nc.scalar.copy
+            for c, copy in ((0, nc.scalar.copy), (ROUND // 2, second)):
                 copy(
                     out=side[:, c * PACK : (c + ROUND // 2) * PACK].rearrange(
                         "p (c i s) -> p c s i", i=4, s=PACK
@@ -230,19 +231,19 @@ def tile_block_pa_t_kernel(
                 out_banks[r].append(out_bank)
 
         def finish_round(r):
+            per_store = 2 if r + 1 < ROUNDS else 1
             for i in range(TILES):
                 nc.vector.tensor_tensor(
                     out=resid[r][:, i, :], in0=out_banks[r][i][:], in1=resid[r][:, i, :], op=ADD
                 )
-                if i % 2 == 1:
+                if (i + 1) % per_store == 0:
+                    first = i + 1 - per_store
                     nc.sync.dma_start(
-                        out=out_dram[r][:, (i - 1) * WIDTH : (i + 1) * WIDTH],
-                        in_=resid[r][:, i - 1 : i + 1, :].rearrange("p i d -> p (i d)"),
+                        out=out_dram[r][:, first * WIDTH : (i + 1) * WIDTH],
+                        in_=resid[r][:, first : i + 1, :].rearrange("p i d -> p (i d)"),
                     )
 
         transpose_round(0)
-        b2_bank = bank("b2_bank")
-        nc.tensor.matmul(out=b2_bank[:], lhsT=ones[:], rhs=b2_rows[:], start=True, stop=True)
         w1_codes, w1_scales = quantise_weight(
             w1_raw[:].rearrange("p j (m s) -> p s m j", s=PACK), "w1"
         )
@@ -251,9 +252,6 @@ def tile_block_pa_t_kernel(
         nc.vector.tensor_copy(out=b1[:], in_=b1_bf16[:])
         regroup("a", 0)
         quantise("a", 0, 1)
-        nc.scalar.copy(out=b2_all[:], in_=b2_bank[:])
-        for r in range(ROUNDS):
-            residual_gpsimd(r)
         wp_codes, wp_scales = quantise_weight(
             wp_raw[:].rearrange("p j (a b) -> p a b j", a=PACK), "wp"
         )
@@ -270,9 +268,18 @@ def tile_block_pa_t_kernel(
                 gelu_round(n)
             if n + 1 < ROUNDS:
                 transpose_round(n + 1)
+                if n == 0:
+                    b2_bank = bank("b2_bank")
+                    nc.tensor.matmul(
+                        out=b2_bank[:], lhsT=ones[:], rhs=b2_rows[:], start=True, stop=True
+                    )
                 regroup("x", n + 1)
                 quantise("x", n + 1, 1)
                 regroup("a", n + 1)
+                if n == 0:
+                    nc.scalar.copy(out=b2_all[:], in_=b2_bank[:])
+                    for r in range(ROUNDS):
+                        residual_gpsimd(r)
             if n >= 1:
                 output_matmuls(n - 1)
                 finish_round(n - 1)

@@ -19,6 +19,7 @@ TOKENS = 4 * 1024
 TILES = 4
 ROUND = TILES * P
 ROUNDS = TOKENS // ROUND
+GPSIMD_TILES = 2
 HALF = WIDTH // 2
 FLOPS = 3 * 2 * TOKENS * WIDTH * WIDTH
 
@@ -51,19 +52,21 @@ def tile_block_pa_t_kernel(
 
         pairs_dram = "(u p e) c -> p u (e c)"
         pairs_sbuf = "p (u e) c -> p u (e c)"
+        nc.sync.dma_start(out=x_sb[0][:], in_=x_dram[0])
         nc.sync.dma_start(
             out=w1_raw[:].rearrange(pairs_sbuf, u=2), in_=w_ff1.rearrange(pairs_dram, u=2, e=2)
         )
-        nc.sync.dma_start(out=x_sb[0][:], in_=x_dram[0])
         nc.sync.dma_start(out=a_sb[0][:], in_=a_dram[0])
         nc.sync.dma_start(
             out=wp_raw[:].rearrange(pairs_sbuf, u=2), in_=w_proj.rearrange(pairs_dram, u=2, e=2)
         )
+        nc.sync.dma_start(out=x_sb[1][:], in_=x_dram[1])
         nc.sync.dma_start(
             out=w2_raw[:].rearrange("p s c -> p (s c)"),
             in_=w_ff2.rearrange("(p s) c -> p (s c)", s=PACK),
         )
-        for r in range(1, ROUNDS):
+        nc.sync.dma_start(out=a_sb[1][:], in_=a_dram[1])
+        for r in range(2, ROUNDS):
             nc.sync.dma_start(out=x_sb[r][:], in_=x_dram[r])
             nc.sync.dma_start(out=a_sb[r][:], in_=a_dram[r])
 
@@ -86,19 +89,24 @@ def tile_block_pa_t_kernel(
         ident = keep.tile([P, P], F32)
         make_identity(nc, ident[:])
 
-        def quantise_weight(raw_view, name):
-            w_grouped = two.tile([P, WIDTH, PACK], BF16, align_bytes=64)
-            codes = keep.tile([P, WIDTH], U32, align_bytes=64, name=name + "_codes")
-            scales = keep.tile([P, WIDTH], U8, align_bytes=64, name=name + "_scales")
+        def regroup_weight(raw_view):
+            w_grouped = two.tile([P, WIDTH * PACK], BF16, align_bytes=64, name="w_grouped")
             nc.vector.tensor_copy(
-                out=w_grouped[:].rearrange("p (a b) j -> p a b j", a=PACK), in_=raw_view
+                out=w_grouped[:].rearrange("p (a b j) -> p a b j", a=PACK, j=PACK), in_=raw_view
             )
-            nc.vector.quantize_mx(
-                out=codes[:].bitcast(FP8X4),
-                scales=scales[:],
-                in_=w_grouped[:].rearrange("p c j -> p (c j)"),
-            )
-            return codes, scales
+            return w_grouped
+
+        def quantise_weight(w_grouped, name, pieces):
+            code = keep.tile([P, WIDTH], U32, align_bytes=64, name=name + "_codes")
+            scale = keep.tile([P, WIDTH], U8, align_bytes=64, name=name + "_scales")
+            step = WIDTH // pieces
+            for c in range(0, WIDTH, step):
+                nc.vector.quantize_mx(
+                    out=code[:, c : c + step].bitcast(FP8X4),
+                    scales=scale[:, c : c + step],
+                    in_=w_grouped[:, c * PACK : (c + step) * PACK],
+                )
+            return code, scale
 
         transposed = {}
         grouped = {}
@@ -174,7 +182,7 @@ def tile_block_pa_t_kernel(
 
         def regroup_hidden(r):
             side = two.tile([P, ROUND * PACK], BF16, align_bytes=64, name="h_grouped")
-            second = nc.vector.tensor_copy if r + 1 < ROUNDS else nc.scalar.copy
+            second = nc.vector.tensor_copy if r + 2 < ROUNDS else nc.scalar.copy
             for c, copy in ((0, nc.scalar.copy), (ROUND // 2, second)):
                 copy(
                     out=side[:, c * PACK : (c + ROUND // 2) * PACK].rearrange(
@@ -187,8 +195,8 @@ def tile_block_pa_t_kernel(
             grouped["h", r] = side
 
         def residual_gpsimd(r):
-            xb = keep.tile([P, TILES, WIDTH], F32, name="resid%d" % r)
-            for i in range(TILES // 2, TILES):
+            xb = three.tile([P, TILES, WIDTH], F32, name="resid")
+            for i in range(GPSIMD_TILES):
                 nc.gpsimd.tensor_tensor(
                     out=xb[:, i, :],
                     in0=x_sb[r][:, i * WIDTH : (i + 1) * WIDTH],
@@ -198,10 +206,11 @@ def tile_block_pa_t_kernel(
             resid[r] = xb
 
         def residual_vector(r):
+            tiles = TILES - GPSIMD_TILES
             nc.vector.tensor_tensor(
-                out=resid[r][:, 0 : TILES // 2, :],
-                in0=x_sb[r][:, 0 : TILES // 2 * WIDTH].rearrange("p (i d) -> p i d", d=WIDTH),
-                in1=b2_all[:].unsqueeze(1).to_broadcast([P, TILES // 2, WIDTH]),
+                out=resid[r][:, GPSIMD_TILES:, :],
+                in0=x_sb[r][:, GPSIMD_TILES * WIDTH :].rearrange("p (i d) -> p i d", d=WIDTH),
+                in1=b2_all[:].unsqueeze(1).to_broadcast([P, tiles, WIDTH]),
                 op=ADD,
             )
 
@@ -244,20 +253,17 @@ def tile_block_pa_t_kernel(
                     )
 
         transpose_round(0)
-        w1_codes, w1_scales = quantise_weight(
-            w1_raw[:].rearrange("p j (m s) -> p s m j", s=PACK), "w1"
-        )
+        w1_grouped = regroup_weight(w1_raw[:].rearrange("p j (m s) -> p s m j", s=PACK))
         regroup("x", 0)
         quantise("x", 0, 1)
+        w1_codes, w1_scales = quantise_weight(w1_grouped, "w1", PACK)
         nc.vector.tensor_copy(out=b1[:], in_=b1_bf16[:])
         regroup("a", 0)
+        wp_grouped = regroup_weight(wp_raw[:].rearrange("p j (a b) -> p a b j", a=PACK))
         quantise("a", 0, 1)
-        wp_codes, wp_scales = quantise_weight(
-            wp_raw[:].rearrange("p j (a b) -> p a b j", a=PACK), "wp"
-        )
-        w2_codes, w2_scales = quantise_weight(
-            w2_raw[:].rearrange("p j (a b) -> p a b j", a=PACK), "w2"
-        )
+        w2_grouped = regroup_weight(w2_raw[:].rearrange("p j (a b) -> p a b j", a=PACK))
+        wp_codes, wp_scales = quantise_weight(wp_grouped, "wp", 1)
+        w2_codes, w2_scales = quantise_weight(w2_grouped, "w2", 1)
 
         for n in range(ROUNDS + 1):
             if n >= 1:
@@ -278,11 +284,13 @@ def tile_block_pa_t_kernel(
                 regroup("a", n + 1)
                 if n == 0:
                     nc.scalar.copy(out=b2_all[:], in_=b2_bank[:])
-                    for r in range(ROUNDS):
+                    for r in range(3):
                         residual_gpsimd(r)
             if n >= 1:
                 output_matmuls(n - 1)
                 finish_round(n - 1)
+                if n + 2 < ROUNDS:
+                    residual_gpsimd(n + 2)
             if n < ROUNDS:
                 regroup_hidden(n)
             if n + 1 < ROUNDS:

@@ -19,7 +19,6 @@ TOKENS = 4 * 1024
 TILES = 4
 ROUND = TILES * P
 ROUNDS = TOKENS // ROUND
-GPSIMD_TILES = 2
 HALF = WIDTH // 2
 FLOPS = 3 * 2 * TOKENS * WIDTH * WIDTH
 
@@ -88,6 +87,8 @@ def tile_block_pa_t_kernel(
 
         ident = keep.tile([P, P], F32)
         make_identity(nc, ident[:])
+        ident_bf16 = keep.tile([P, P], BF16)
+        make_identity(nc, ident_bf16[:])
 
         def regroup_weight(raw_view):
             w_grouped = two.tile([P, WIDTH * PACK], BF16, align_bytes=64, name="w_grouped")
@@ -182,37 +183,47 @@ def tile_block_pa_t_kernel(
 
         def regroup_hidden(r):
             side = two.tile([P, ROUND * PACK], BF16, align_bytes=64, name="h_grouped")
-            second = nc.vector.tensor_copy if r + 2 < ROUNDS else nc.scalar.copy
-            for c, copy in ((0, nc.scalar.copy), (ROUND // 2, second)):
+            if r + 2 < ROUNDS:
+                parts = ((0, P, nc.scalar.copy), (P, ROUND, nc.vector.tensor_copy))
+            else:
+                parts = ((0, ROUND // 2, nc.scalar.copy), (ROUND // 2, ROUND, nc.scalar.copy))
+            for c, end, copy in parts:
                 copy(
-                    out=side[:, c * PACK : (c + ROUND // 2) * PACK].rearrange(
+                    out=side[:, c * PACK : end * PACK].rearrange(
                         "p (c i s) -> p c s i", i=4, s=PACK
                     ),
-                    in_=h_planes[r][:, :, c : c + ROUND // 2].rearrange(
-                        "p s (c i) -> p c s i", i=4
-                    ),
+                    in_=h_planes[r][:, :, c:end].rearrange("p s (c i) -> p c s i", i=4),
                 )
             grouped["h", r] = side
 
         def residual_gpsimd(r):
             xb = three.tile([P, TILES, WIDTH], F32, name="resid")
-            for i in range(GPSIMD_TILES):
-                nc.gpsimd.tensor_tensor(
-                    out=xb[:, i, :],
-                    in0=x_sb[r][:, i * WIDTH : (i + 1) * WIDTH],
-                    in1=b2_all[:],
-                    op=ADD,
-                )
+            nc.gpsimd.tensor_tensor(
+                out=xb[:, 0, :], in0=x_sb[r][:, 0:WIDTH], in1=b2_all[:], op=ADD
+            )
             resid[r] = xb
 
         def residual_vector(r):
-            tiles = TILES - GPSIMD_TILES
             nc.vector.tensor_tensor(
-                out=resid[r][:, GPSIMD_TILES:, :],
-                in0=x_sb[r][:, GPSIMD_TILES * WIDTH :].rearrange("p (i d) -> p i d", d=WIDTH),
-                in1=b2_all[:].unsqueeze(1).to_broadcast([P, tiles, WIDTH]),
+                out=resid[r][:, 1:3, :],
+                in0=x_sb[r][:, WIDTH : 3 * WIDTH].rearrange("p (i d) -> p i d", d=WIDTH),
+                in1=b2_all[:].unsqueeze(1).to_broadcast([P, 2, WIDTH]),
                 op=ADD,
             )
+
+        def residual_tensor(r):
+            resid_bank = bank("resid_bank")
+            nc.tensor.matmul(
+                out=resid_bank[:],
+                lhsT=ident_bf16[:],
+                rhs=x_sb[r][:, 3 * WIDTH : 4 * WIDTH],
+                start=True,
+                stop=False,
+            )
+            nc.tensor.matmul(
+                out=resid_bank[:], lhsT=ones[:], rhs=b2_rows[:], start=False, stop=True
+            )
+            return resid_bank
 
         def output_matmuls(r):
             out_banks[r] = []
@@ -286,6 +297,9 @@ def tile_block_pa_t_kernel(
                     nc.scalar.copy(out=b2_all[:], in_=b2_bank[:])
                     for r in range(3):
                         residual_gpsimd(r)
+            if n < ROUNDS:
+                resid_bank = residual_tensor(n)
+                nc.scalar.copy(out=resid[n][:, 3, :], in_=resid_bank[:])
             if n >= 1:
                 output_matmuls(n - 1)
                 finish_round(n - 1)

@@ -183,7 +183,12 @@ def tile_block_pa_t_kernel(
 
         def regroup_hidden(r):
             side = two.tile([P, ROUND * PACK], BF16, align_bytes=64, name="h_grouped")
-            if r + 2 < ROUNDS:
+            if r == 0:
+                parts = (
+                    (0, ROUND // 2, nc.vector.tensor_copy),
+                    (ROUND // 2, ROUND, nc.vector.tensor_copy),
+                )
+            elif r + 2 < ROUNDS:
                 parts = ((0, P, nc.scalar.copy), (P, ROUND, nc.vector.tensor_copy))
             else:
                 parts = ((0, ROUND // 2, nc.scalar.copy), (ROUND // 2, ROUND, nc.scalar.copy))
@@ -198,9 +203,13 @@ def tile_block_pa_t_kernel(
 
         def residual_gpsimd(r):
             xb = three.tile([P, TILES, WIDTH], F32, name="resid")
-            nc.gpsimd.tensor_tensor(
-                out=xb[:, 0, :], in0=x_sb[r][:, 0:WIDTH], in1=b2_all[:], op=ADD
-            )
+            for i in range(1 if r + 1 < ROUNDS else 3):
+                nc.gpsimd.tensor_tensor(
+                    out=xb[:, i, :],
+                    in0=x_sb[r][:, i * WIDTH : (i + 1) * WIDTH],
+                    in1=b2_all[:],
+                    op=ADD,
+                )
             resid[r] = xb
 
         def residual_vector(r):
@@ -279,7 +288,8 @@ def tile_block_pa_t_kernel(
         for n in range(ROUNDS + 1):
             if n >= 1:
                 quantise("h", n - 1, 2)
-                residual_vector(n - 1)
+                if n < ROUNDS:
+                    residual_vector(n - 1)
             if n < ROUNDS:
                 hidden_matmuls(n)
                 gelu_round(n)

from contextlib import ExitStack

import concourse.mybir as mybir
from concourse.masks import make_identity

F32 = mybir.dt.float32
BF16 = mybir.dt.bfloat16
I32 = mybir.dt.int32
U32 = mybir.dt.uint32
U8 = mybir.dt.uint8
FP8X4 = mybir.dt.float8_e4m3fn_x4
GELU = mybir.ActivationFunctionType.Gelu
ADD = mybir.AluOpType.add

P = 128
PACK = 4
WIDTH = P * PACK
TOKENS = 4 * 1024
TILES = 4
ROUND = TILES * P
ROUNDS = TOKENS // ROUND
HALF = WIDTH // 2
FLOPS = 3 * 2 * TOKENS * WIDTH * WIDTH


def tile_block_pa_t_kernel(
    tc, x, attn_merged, w_proj, w_ff1, b_ff1, w_ff2, b_ff2, out
):
    nc = tc.nc

    by_round = "(r p i) d -> r p (i d)"
    x_dram = x.flatten_outer_dims().rearrange(by_round, p=P, i=TILES)
    a_dram = attn_merged.flatten_outer_dims().rearrange(by_round, p=P, i=TILES)
    out_dram = out.flatten_outer_dims().rearrange(by_round, p=P, i=TILES)

    with ExitStack() as ctx:
        keep = ctx.enter_context(tc.tile_pool(name="keep", bufs=1))
        two = ctx.enter_context(tc.tile_pool(name="two", bufs=2))
        three = ctx.enter_context(tc.tile_pool(name="three", bufs=3))
        psum = ctx.enter_context(tc.psum_pool(name="psum", bufs=8))
        ctx.enter_context(tc.manual_schedule())

        def bank(name):
            return psum.tile([P, WIDTH], F32, name=name, tag="bank")

        x_sb = [keep.tile([P, TILES * WIDTH], BF16, name="x%d" % r) for r in range(ROUNDS)]
        a_sb = [keep.tile([P, TILES * WIDTH], BF16, name="a%d" % r) for r in range(ROUNDS)]
        w1_raw = keep.tile([P, PACK, WIDTH], BF16)
        wp_raw = keep.tile([P, PACK, WIDTH], BF16)
        w2_raw = keep.tile([P, PACK, WIDTH], BF16)

        pairs_dram = "(u p e) c -> p u (e c)"
        pairs_sbuf = "p (u e) c -> p u (e c)"
        nc.sync.dma_start(out=x_sb[0][:], in_=x_dram[0])
        nc.sync.dma_start(
            out=w1_raw[:].rearrange(pairs_sbuf, u=2), in_=w_ff1.rearrange(pairs_dram, u=2, e=2)
        )
        nc.sync.dma_start(out=a_sb[0][:], in_=a_dram[0])
        nc.sync.dma_start(
            out=wp_raw[:].rearrange(pairs_sbuf, u=2), in_=w_proj.rearrange(pairs_dram, u=2, e=2)
        )
        nc.sync.dma_start(out=x_sb[1][:], in_=x_dram[1])
        nc.sync.dma_start(
            out=w2_raw[:].rearrange("p s c -> p (s c)"),
            in_=w_ff2.rearrange("(p s) c -> p (s c)", s=PACK),
        )
        nc.sync.dma_start(out=a_sb[1][:], in_=a_dram[1])
        for r in range(2, ROUNDS):
            nc.sync.dma_start(out=x_sb[r][:], in_=x_dram[r])
            nc.sync.dma_start(out=a_sb[r][:], in_=a_dram[r])

        b1_bf16 = keep.tile([P, PACK], BF16)
        b1 = keep.tile([P, PACK], F32)
        nc.scalar.dma_start(out=b1_bf16[:], in_=b_ff1.rearrange("(p s) -> p s", s=PACK))

        ones = keep.tile([P, P], BF16)
        b2_rows = keep.tile([P, WIDTH], BF16)
        b2_all = keep.tile([P, WIDTH], BF16)
        nc.vector.memset(b2_rows[:].bitcast(I32), 0)
        nc.vector.memset(ones[:], 1.0)
        nc.scalar.dma_start(out=b2_rows[0:1, :], in_=b_ff2.unsqueeze(0))

        warm = keep.tile([P, 1], F32)
        warm_out = keep.tile([P, 1], F32)
        nc.vector.memset(warm[:], 0.0)
        nc.scalar.activation(out=warm_out[:], in_=warm[:], func=GELU)

        ident = keep.tile([P, P], F32)
        make_identity(nc, ident[:])
        ident_bf16 = keep.tile([P, P], BF16)
        make_identity(nc, ident_bf16[:])

        def regroup_weight(raw_view):
            w_grouped = two.tile([P, WIDTH * PACK], BF16, align_bytes=64, name="w_grouped")
            nc.vector.tensor_copy(
                out=w_grouped[:].rearrange("p (a b j) -> p a b j", a=PACK, j=PACK), in_=raw_view
            )
            return w_grouped

        def quantise_weight(w_grouped, name, pieces):
            code = keep.tile([P, WIDTH], U32, align_bytes=64, name=name + "_codes")
            scale = keep.tile([P, WIDTH], U8, align_bytes=64, name=name + "_scales")
            step = WIDTH // pieces
            for c in range(0, WIDTH, step):
                nc.vector.quantize_mx(
                    out=code[:, c : c + step].bitcast(FP8X4),
                    scales=scale[:, c : c + step],
                    in_=w_grouped[:, c * PACK : (c + step) * PACK],
                )
            return code, scale

        transposed = {}
        grouped = {}
        codes = {}
        scales = {}
        h_banks = {}
        h_planes = {}
        out_banks = {}
        resid = {}

        def transpose_round(r):
            for name, src in (("x", x_sb[r]), ("a", a_sb[r])):
                transposed[name, r] = []
                for half in range(2):
                    words_t = bank("words_t")
                    for i in range(2):
                        tile_i = 2 * half + i
                        words = src[:, tile_i * WIDTH : (tile_i + 1) * WIDTH].bitcast(F32)
                        for u in range(2):
                            nc.tensor.transpose(
                                out=words_t[:, u * HALF + i * P : u * HALF + (i + 1) * P],
                                in_=words[:, u * P : (u + 1) * P],
                                identity=ident[:],
                            )
                    transposed[name, r].append(words_t)

        def regroup(name, r):
            side = two.tile([P, ROUND * PACK], BF16, align_bytes=64, name=name + "_grouped")
            for half, words_t in enumerate(transposed[name, r]):
                nc.scalar.copy(
                    out=side[:, half * 2 * WIDTH : (half + 1) * 2 * WIDTH]
                    .bitcast(F32)
                    .rearrange("p (c u) -> p c u", u=2),
                    in_=words_t[:].rearrange("p (u c) -> p c u", u=2),
                )
            grouped[name, r] = side

        def quantise(name, r, pieces):
            code = three.tile([P, ROUND], U32, align_bytes=64, name=name + "_codes")
            scale = three.tile([P, ROUND], U8, align_bytes=64, name=name + "_scales")
            step = ROUND // pieces
            for c in range(0, ROUND, step):
                nc.vector.quantize_mx(
                    out=code[:, c : c + step].bitcast(FP8X4),
                    scales=scale[:, c : c + step],
                    in_=grouped[name, r][:, c * PACK : (c + step) * PACK],
                )
            codes[name, r] = code
            scales[name, r] = scale

        def hidden_matmuls(r):
            h_banks[r] = []
            for s in range(PACK):
                h_bank = bank("h_bank")
                nc.tensor.matmul_mx(
                    out=h_bank[:],
                    lhsT=w1_codes[:, s * P : (s + 1) * P].bitcast(FP8X4),
                    lhsT_scale=w1_scales[:, s * P : (s + 1) * P],
                    rhs=codes["x", r][:].bitcast(FP8X4),
                    rhs_scale=scales["x", r][:],
                    start=True,
                    stop=True,
                )
                h_banks[r].append(h_bank)

        def gelu_round(r):
            planes = two.tile([P, PACK, ROUND], BF16, name="h_planes")
            for s in range(PACK):
                nc.scalar.activation(
                    out=planes[:, s, :], in_=h_banks[r][s][:], func=GELU, bias=b1[:, s : s + 1]
                )
            h_planes[r] = planes

        def regroup_hidden(r):
            side = two.tile([P, ROUND * PACK], BF16, align_bytes=64, name="h_grouped")
            if r == 0:
                parts = (
                    (0, ROUND // 2, nc.vector.tensor_copy),
                    (ROUND // 2, ROUND, nc.vector.tensor_copy),
                )
            elif r + 2 < ROUNDS:
                parts = ((0, P, nc.scalar.copy), (P, ROUND, nc.vector.tensor_copy))
            else:
                parts = ((0, ROUND // 2, nc.scalar.copy), (ROUND // 2, ROUND, nc.scalar.copy))
            for c, end, copy in parts:
                copy(
                    out=side[:, c * PACK : end * PACK].rearrange(
                        "p (c i s) -> p c s i", i=4, s=PACK
                    ),
                    in_=h_planes[r][:, :, c:end].rearrange("p s (c i) -> p c s i", i=4),
                )
            grouped["h", r] = side

        def residual_gpsimd(r):
            xb = three.tile([P, TILES, WIDTH], F32, name="resid")
            for i in range(1 if r + 1 < ROUNDS else 3):
                nc.gpsimd.tensor_tensor(
                    out=xb[:, i, :],
                    in0=x_sb[r][:, i * WIDTH : (i + 1) * WIDTH],
                    in1=b2_all[:],
                    op=ADD,
                )
            resid[r] = xb

        def residual_vector(r):
            nc.vector.tensor_tensor(
                out=resid[r][:, 1:3, :],
                in0=x_sb[r][:, WIDTH : 3 * WIDTH].rearrange("p (i d) -> p i d", d=WIDTH),
                in1=b2_all[:].unsqueeze(1).to_broadcast([P, 2, WIDTH]),
                op=ADD,
            )

        def residual_tensor(r):
            resid_bank = bank("resid_bank")
            nc.tensor.matmul(
                out=resid_bank[:],
                lhsT=ident_bf16[:],
                rhs=x_sb[r][:, 3 * WIDTH : 4 * WIDTH],
                start=True,
                stop=False,
            )
            nc.tensor.matmul(
                out=resid_bank[:], lhsT=ones[:], rhs=b2_rows[:], start=False, stop=True
            )
            return resid_bank

        def output_matmuls(r):
            out_banks[r] = []
            for i in range(TILES):
                tile_cols = slice(i * P, (i + 1) * P)
                out_bank = bank("out_bank")
                nc.tensor.matmul_mx(
                    out=out_bank[:],
                    lhsT=codes["a", r][:, tile_cols].bitcast(FP8X4),
                    lhsT_scale=scales["a", r][:, tile_cols],
                    rhs=wp_codes[:].bitcast(FP8X4),
                    rhs_scale=wp_scales[:],
                    start=True,
                    stop=False,
                )
                nc.tensor.matmul_mx(
                    out=out_bank[:],
                    lhsT=codes["h", r][:, tile_cols].bitcast(FP8X4),
                    lhsT_scale=scales["h", r][:, tile_cols],
                    rhs=w2_codes[:].bitcast(FP8X4),
                    rhs_scale=w2_scales[:],
                    start=False,
                    stop=True,
                )
                out_banks[r].append(out_bank)

        def finish_round(r):
            per_store = 2 if r + 1 < ROUNDS else 1
            for i in range(TILES):
                nc.vector.tensor_tensor(
                    out=resid[r][:, i, :], in0=out_banks[r][i][:], in1=resid[r][:, i, :], op=ADD
                )
                if (i + 1) % per_store == 0:
                    first = i + 1 - per_store
                    nc.sync.dma_start(
                        out=out_dram[r][:, first * WIDTH : (i + 1) * WIDTH],
                        in_=resid[r][:, first : i + 1, :].rearrange("p i d -> p (i d)"),
                    )

        transpose_round(0)
        w1_grouped = regroup_weight(w1_raw[:].rearrange("p j (m s) -> p s m j", s=PACK))
        regroup("x", 0)
        quantise("x", 0, 1)
        w1_codes, w1_scales = quantise_weight(w1_grouped, "w1", PACK)
        nc.vector.tensor_copy(out=b1[:], in_=b1_bf16[:])
        regroup("a", 0)
        wp_grouped = regroup_weight(wp_raw[:].rearrange("p j (a b) -> p a b j", a=PACK))
        quantise("a", 0, 1)
        w2_grouped = regroup_weight(w2_raw[:].rearrange("p j (a b) -> p a b j", a=PACK))
        wp_codes, wp_scales = quantise_weight(wp_grouped, "wp", 1)
        w2_codes, w2_scales = quantise_weight(w2_grouped, "w2", 1)

        for n in range(ROUNDS + 1):
            if n >= 1:
                quantise("h", n - 1, 2)
                if n < ROUNDS:
                    residual_vector(n - 1)
            if n < ROUNDS:
                hidden_matmuls(n)
                gelu_round(n)
            if n + 1 < ROUNDS:
                transpose_round(n + 1)
                if n == 0:
                    b2_bank = bank("b2_bank")
                    nc.tensor.matmul(
                        out=b2_bank[:], lhsT=ones[:], rhs=b2_rows[:], start=True, stop=True
                    )
                regroup("x", n + 1)
                quantise("x", n + 1, 1)
                regroup("a", n + 1)
                if n == 0:
                    nc.scalar.copy(out=b2_all[:], in_=b2_bank[:])
                    for r in range(3):
                        residual_gpsimd(r)
            if n < ROUNDS:
                resid_bank = residual_tensor(n)
                nc.scalar.copy(out=resid[n][:, 3, :], in_=resid_bank[:])
            if n >= 1:
                output_matmuls(n - 1)
                finish_round(n - 1)
                if n + 2 < ROUNDS:
                    residual_gpsimd(n + 2)
            if n < ROUNDS:
                regroup_hidden(n)
            if n + 1 < ROUNDS:
                quantise("a", n + 1, 1)
